import numpy as np
import ml_dtypes


def mxq(x, axis, fmt="e4m3"):
    dtype, down = {"e4m3": (ml_dtypes.float8_e4m3fn, 7), "e5m2": (ml_dtypes.float8_e5m2, 14)}[fmt]
    v = np.moveaxis(np.asarray(x, np.float32).astype(ml_dtypes.bfloat16).astype(np.float64), axis, -1)
    blocks = v.reshape(v.shape[:-1] + (-1, 32))
    amax = np.abs(blocks).max(-1, keepdims=True)
    byte = np.maximum(np.where(amax > 0, np.frexp(amax)[1] - 1 + 127, 0) - down, 1)
    scale = np.exp2(byte - 127.0)
    codes = (blocks / scale).astype(np.float32).astype(dtype).astype(np.float64)
    return np.moveaxis((codes * scale).reshape(v.shape), -1, axis)


WIDE = False


def mx_kscale(k):
    if not WIDE:
        return np.ones(k)
    levels = np.array([10, -10, 5, -5, 0])
    a = np.random.permutation(np.resize(levels, k // 512 * 4)).reshape(k // 512, 4)
    idx = np.arange(k)
    return np.exp2(a[idx // 512, idx % 128 // 32])


BF16 = ml_dtypes.bfloat16


def bf(x):
    return np.asarray(x, np.float32).astype(BF16)


def f64(x):
    return np.asarray(x).astype(np.float64)


E2M1 = np.array([0.0, 0.5, 1.0, 1.5, 2.0, 3.0, 4.0, 6.0, -0.0, -0.5, -1.0, -1.5, -2.0, -3.0, -4.0, -6.0])


def pack_weight(w, fmt):
    k, n = w.shape
    w = f64(bf(w)).reshape(k // 32, 32, n)
    amax = np.abs(w).max(1)
    if fmt == "e4m3":
        byte = np.frexp(amax)[1] - 1 + 127 - 7
    else:
        mant, ex = np.frexp(amax / 6.0)
        byte = np.where(mant > 0.5, ex, ex - 1) + 127
    byte = np.clip(np.where(amax > 0, byte, 1), 1, 254)
    scaled = (w * np.exp2(127.0 - byte)[:, None, :]).reshape(k, n).astype(np.float32)
    by_word = np.ascontiguousarray(scaled.reshape(k // 512, 128, 4, n).transpose(0, 1, 3, 2))
    if fmt == "e4m3":
        words = by_word.astype(ml_dtypes.float8_e4m3fn).view(np.uint8)
    else:
        c = by_word.astype(ml_dtypes.float4_e2m1fn).view(np.uint8) & 0xF
        words = c[..., 0::2] | (c[..., 1::2] << 4)
    return np.ascontiguousarray(words), np.ascontiguousarray(byte.astype(np.uint8).reshape(k // 512, 16, n))


def unpack_weight(words, scales, fmt):
    g, p, n, _ = words.shape
    if fmt == "e4m3":
        vals = np.ascontiguousarray(words).view(ml_dtypes.float8_e4m3fn).astype(np.float64)
    else:
        nib = np.empty((g, p, n, 4), np.uint8)
        nib[..., 0::2] = words & 0xF
        nib[..., 1::2] = words >> 4
        vals = E2M1[nib]
    vals = vals * np.repeat(np.exp2(scales.astype(np.float64) - 127.0), 8, axis=1)[..., None]
    return vals.transpose(0, 1, 3, 2).reshape(g * 512, n)

def pack4(w):
    words, scales = pack_weight(w, "e2m1")
    return words.reshape(words.shape[0], 128, -1), scales


def unpack4(words, scales):
    return unpack_weight(words.reshape(words.shape[0], 128, -1, 2), scales, "e2m1")


B, S, D, E, H = 2, 128, 16384, 512, 2
DH = E // H
ROPE_BASE = 10000.0


def rope_tables():
    inv_freq = 1.0 / (ROPE_BASE ** (np.arange(0, DH, 2) / DH))
    freqs = np.arange(S)[:, None] * inv_freq[None, :]
    emb = np.concatenate([freqs, freqs], axis=-1)
    return np.cos(emb), np.sin(emb)


def rotate(y, cos, sin):
    y1, y2 = y[..., :DH], y[..., DH:]
    return np.concatenate([y1 * cos - y2 * sin, y2 * cos + y1 * sin], axis=-1)


def setup_inputs():
    s = mx_kscale(D)
    cos, sin = rope_tables()
    x = bf(np.random.standard_normal((B, S, D)) * s)
    wq_words, wq_scales = pack4(np.random.standard_normal((D, E)) / np.sqrt(D) / s[:, None])
    wk_words, wk_scales = pack4(np.random.standard_normal((D, E)) / np.sqrt(D) / s[:, None])
    return {"x": x,
            "wq_words": wq_words, "wq_scales": wq_scales,
            "wk_words": wk_words, "wk_scales": wk_scales,
            "cos": bf(cos), "sin": bf(sin)}


def reference(x, wq_words, wq_scales, wk_words, wk_scales, cos, sin):
    xq = mxq(f64(x), 2, "e4m3")
    q = xq @ unpack4(wq_words, wq_scales)
    k = xq @ unpack4(wk_words, wk_scales)
    c, sn = f64(cos), f64(sin)
    q_rot = rotate(q, c, sn).reshape(B, S, H, DH).transpose(0, 2, 1, 3)
    k_rot = rotate(k, c, sn).reshape(B, S, H, DH).transpose(0, 2, 1, 3)
    return q_rot, k_rot

@@ -1,0 +1,227 @@
+from contextlib import ExitStack
+
+import concourse.masks as masks
+import concourse.mybir as mybir
+
+F32 = mybir.dt.float32
+BF16 = mybir.dt.bfloat16
+I32 = mybir.dt.int32
+U32 = mybir.dt.uint32
+U8 = mybir.dt.uint8
+FP8X4 = mybir.dt.float8_e4m3fn_x4
+FP4X4 = mybir.dt.float4_e2m1fn_x4
+MULT = mybir.AluOpType.mult
+ADD = mybir.AluOpType.add
+SUBTRACT = mybir.AluOpType.subtract
+
+P = 128
+PACK = 4
+K_PASS = P * PACK
+BATCH = 2
+SEQ = 128
+D_MODEL = 16384
+CHANNELS = 512
+HEAD = CHANNELS // 2
+PASSES = D_MODEL // K_PASS
+WORDS = K_PASS // 2
+
+ROUND = 4
+ROUNDS = PASSES // ROUND
+K_LAG = 1
+LOAD_AHEAD = 3
+SCALE_ROUNDS = 2
+SCALE_PASSES = SCALE_ROUNDS * ROUND
+
+FLOPS = 2 * BATCH * SEQ * D_MODEL * 2 * CHANNELS
+
+
+def tile_multiheadattention_pa_k_kernel(
+    tc, x, wq_words, wq_scales, wk_words, wk_scales, cos, sin, out_0, out_1
+):
+    nc = tc.nc
+    weights = ("q", "k")
+    words_in = {"q": wq_words, "k": wk_words}
+    scales_in = {"q": wq_scales, "k": wk_scales}
+    outputs = {"q": out_0, "k": out_1}
+
+    with ExitStack() as ctx:
+        keep = ctx.enter_context(tc.tile_pool(name="keep", bufs=1))
+        x_pool = ctx.enter_context(tc.tile_pool(name="x_pool", bufs=LOAD_AHEAD + 1))
+        sorted_pool = ctx.enter_context(tc.tile_pool(name="sorted_pool", bufs=2))
+        grouped_pool = ctx.enter_context(tc.tile_pool(name="grouped_pool", bufs=2))
+        words_pool = ctx.enter_context(tc.tile_pool(name="words_pool", bufs=LOAD_AHEAD + 1))
+        rot_pool = ctx.enter_context(tc.tile_pool(name="rot_pool", bufs=2))
+        sums_pool = ctx.enter_context(tc.psum_pool(name="sums_pool", bufs=1))
+        xt_pool = ctx.enter_context(tc.psum_pool(name="xt_pool", bufs=ROUND))
+        ctx.enter_context(tc.manual_schedule())
+
+        identity = keep.tile([P, P], F32, name="identity")
+        cos_sb = keep.tile([P, HEAD], BF16, name="cos_sb")
+        sin_sb = keep.tile([P, HEAD], BF16, name="sin_sb")
+        x_codes = keep.tile([P, PASSES, BATCH, SEQ], U32, name="x_codes", align_bytes=64)
+        x_scales = keep.tile([P, PASSES, BATCH, SEQ], U8, name="x_scales", align_bytes=64)
+        w_planes = {
+            w: keep.tile([P, PASSES, CHANNELS], U8, name="planes_" + w, align_bytes=64)
+            for w in weights
+        }
+        sums = {
+            (w, b): sums_pool.tile([P, CHANNELS], F32, name="sums_%s%d" % (w, b))
+            for w in weights
+            for b in range(BATCH)
+        }
+
+        x_raw = {}
+        x_sorted = {}
+        x_grouped = {}
+        w_words = {}
+
+        def load_x(r):
+            x_raw[r] = x_pool.tile([P, BATCH, ROUND * K_PASS], BF16, name="x_raw")
+            for b in range(BATCH):
+                nc.sync.dma_start(
+                    out=x_raw[r][:, b, :],
+                    in_=x[b, :, r * ROUND * K_PASS : (r + 1) * ROUND * K_PASS],
+                )
+
+        def load_scales(group):
+            first = group * SCALE_PASSES
+            for w in weights:
+                rows = scales_in[w].bitcast(I32).rearrange("g (qq r) n -> r qq g n", r=4)
+                for r4 in range(4):
+                    for half in range(2):
+                        nc.sync.dma_start(
+                            out=w_planes[w][
+                                32 * half + r4 : P : 64, first : first + SCALE_PASSES, :
+                            ].bitcast(I32),
+                            in_=rows[r4, half:4:2, first : first + SCALE_PASSES, :],
+                        )
+
+        def load_words(w, r):
+            w_words[w, r] = words_pool.tile(
+                [P, ROUND, 2 * CHANNELS], U8, name="words_" + w, align_bytes=64
+            )
+            nc.sync.dma_start(
+                out=w_words[w, r][:].bitcast(I32),
+                in_=words_in[w][r * ROUND : (r + 1) * ROUND]
+                .bitcast(I32)
+                .rearrange("g p n -> p g n"),
+            )
+
+        def load_step(j):
+            if j + 1 < ROUNDS:
+                load_x(j + 1)
+            if j < ROUNDS and j % SCALE_ROUNDS == 0:
+                load_scales(j // SCALE_ROUNDS)
+            if j < ROUNDS:
+                load_words("q", j)
+            if K_LAG <= j < ROUNDS + K_LAG:
+                load_words("k", j - K_LAG)
+
+        def sort_words(r):
+            x_sorted[r] = sorted_pool.tile([P, BATCH, ROUND, 2, P], F32, name="x_sorted")
+            nc.vector.tensor_copy(
+                out=x_sorted[r][:],
+                in_=x_raw[r][:]
+                .bitcast(F32)
+                .rearrange("s b (g p u) -> s b g u p", g=ROUND, u=2),
+            )
+
+        def transpose_round(r):
+            x_grouped[r] = grouped_pool.tile(
+                [P, ROUND, BATCH, SEQ, PACK], BF16, name="x_grouped", align_bytes=64
+            )
+            grouped_words = x_grouped[r][:].bitcast(F32)
+            for g in range(ROUND):
+                xt = xt_pool.tile([P, BATCH, 2, SEQ], F32, name="xt")
+                for b in range(BATCH):
+                    for u in range(2):
+                        nc.tensor.transpose(xt[:, b, u, :], x_sorted[r][:, b, g, u, :], identity[:])
+                nc.scalar.copy(
+                    out=grouped_words[:, g], in_=xt[:].rearrange("p b u s -> p b s u")
+                )
+
+        def quantise_round(r):
+            passes = slice(r * ROUND, (r + 1) * ROUND)
+            nc.vector.quantize_mx(
+                out=x_codes[:, passes].rearrange("p g b s -> p (g b s)").bitcast(FP8X4),
+                scales=x_scales[:, passes].rearrange("p g b s -> p (g b s)"),
+                in_=x_grouped[r][:].rearrange("p g b s t -> p (g b s t)"),
+            )
+
+        def multiply_round(w, r):
+            for b in range(BATCH):
+                for g in range(r * ROUND, (r + 1) * ROUND):
+                    nc.tensor.matmul_mx(
+                        out=sums[w, b][:],
+                        lhsT=x_codes[:, g, b, :].bitcast(FP8X4),
+                        lhsT_scale=x_scales[:, g, b, :],
+                        rhs=w_words[w, r][:, g - r * ROUND, :].bitcast(FP4X4),
+                        rhs_scale=w_planes[w][:, g, :],
+                        start=(g == 0),
+                        stop=(g == PASSES - 1),
+                    )
+
+        def rotate_and_store(w):
+            by_cos = {}
+            by_sin = {}
+            for b in range(BATCH):
+                heads = sums[w, b][:].rearrange("s (h c) -> s h c", h=2)
+                by_cos[b] = rot_pool.tile([P, 2, HEAD], F32, name="by_cos")
+                by_sin[b] = rot_pool.tile([P, 2, HEAD], F32, name="by_sin")
+                nc.vector.tensor_tensor(
+                    out=by_cos[b][:],
+                    in0=heads,
+                    in1=cos_sb[:].unsqueeze(1).to_broadcast([P, 2, HEAD]),
+                    op=MULT,
+                )
+                nc.vector.tensor_tensor(
+                    out=by_sin[b][:],
+                    in0=heads,
+                    in1=sin_sb[:].unsqueeze(1).to_broadcast([P, 2, HEAD]),
+                    op=MULT,
+                )
+            for b in range(BATCH):
+                rotated = rot_pool.tile([P, 2, HEAD], F32, name="rotated")
+                nc.vector.tensor_tensor(
+                    out=rotated[:, 0, :], in0=by_cos[b][:, 0, :], in1=by_sin[b][:, 1, :], op=SUBTRACT
+                )
+                nc.vector.tensor_tensor(
+                    out=rotated[:, 1, :], in0=by_cos[b][:, 1, :], in1=by_sin[b][:, 0, :], op=ADD
+                )
+                nc.sync.dma_start(out=outputs[w][b].rearrange("h s c -> s h c"), in_=rotated[:])
+
+        masks.make_identity(nc, identity[:])
+        nc.scalar.dma_start(out=cos_sb[:], in_=cos)
+        nc.scalar.dma_start(out=sin_sb[:], in_=sin)
+        for group in range(ROUNDS // SCALE_ROUNDS):
+            for w in weights:
+                nc.vector.memset(
+                    w_planes[w][
+                        :, group * SCALE_PASSES : (group + 1) * SCALE_PASSES, :
+                    ].bitcast(I32),
+                    0,
+                )
+
+        load_x(0)
+        for j in range(LOAD_AHEAD):
+            load_step(j)
+        sort_words(0)
+        transpose_round(0)
+        quantise_round(0)
+        sort_words(1)
+
+        for s in range(ROUNDS + K_LAG):
+            load_step(s + LOAD_AHEAD)
+            if s + 1 < ROUNDS:
+                transpose_round(s + 1)
+            if s < ROUNDS:
+                multiply_round("q", s)
+            if s >= K_LAG:
+                multiply_round("k", s - K_LAG)
+            if s + 1 < ROUNDS:
+                quantise_round(s + 1)
+            if s + 2 < ROUNDS:
+                sort_words(s + 2)
+            if s == ROUNDS - 1:
+                rotate_and_store("q")
+        rotate_and_store("k")

@@ -29,7 +29,7 @@ ROUND = 4
 ROUNDS = PASSES // ROUND
 K_LAG = 1
 LOAD_AHEAD = 3
-SCALE_ROUNDS = 2
+SCALE_ROUNDS = ROUNDS // 2
 SCALE_PASSES = SCALE_ROUNDS * ROUND
 
 FLOPS = 2 * BATCH * SEQ * D_MODEL * 2 * CHANNELS
@@ -47,7 +47,7 @@ def tile_multiheadattention_pa_k_kernel(
     with ExitStack() as ctx:
         keep = ctx.enter_context(tc.tile_pool(name="keep", bufs=1))
         x_pool = ctx.enter_context(tc.tile_pool(name="x_pool", bufs=LOAD_AHEAD + 1))
-        sorted_pool = ctx.enter_context(tc.tile_pool(name="sorted_pool", bufs=2))
+        sorted_pool = ctx.enter_context(tc.tile_pool(name="sorted_pool", bufs=3))
         grouped_pool = ctx.enter_context(tc.tile_pool(name="grouped_pool", bufs=2))
         words_pool = ctx.enter_context(tc.tile_pool(name="words_pool", bufs=LOAD_AHEAD + 1))
         rot_pool = ctx.enter_context(tc.tile_pool(name="rot_pool", bufs=2))
@@ -83,18 +83,14 @@ def tile_multiheadattention_pa_k_kernel(
                     in_=x[b, :, r * ROUND * K_PASS : (r + 1) * ROUND * K_PASS],
                 )
 
-        def load_scales(group):
-            first = group * SCALE_PASSES
-            for w in weights:
-                rows = scales_in[w].bitcast(I32).rearrange("g (qq r) n -> r qq g n", r=4)
-                for r4 in range(4):
-                    for half in range(2):
-                        nc.sync.dma_start(
-                            out=w_planes[w][
-                                32 * half + r4 : P : 64, first : first + SCALE_PASSES, :
-                            ].bitcast(I32),
-                            in_=rows[r4, half:4:2, first : first + SCALE_PASSES, :],
-                        )
+        def load_scales(w, half):
+            first = half * SCALE_PASSES
+            rows = scales_in[w].bitcast(I32).rearrange("g (qq r) n -> r qq g n", r=4)
+            for r4 in range(4):
+                nc.sync.dma_start(
+                    out=w_planes[w][r4:P:32, first : first + SCALE_PASSES, :].bitcast(I32),
+                    in_=rows[r4, :, first : first + SCALE_PASSES, :],
+                )
 
         def load_words(w, r):
             w_words[w, r] = words_pool.tile(
@@ -110,12 +106,11 @@ def tile_multiheadattention_pa_k_kernel(
         def load_step(j):
             if j + 1 < ROUNDS:
                 load_x(j + 1)
-            if j < ROUNDS and j % SCALE_ROUNDS == 0:
-                load_scales(j // SCALE_ROUNDS)
-            if j < ROUNDS:
-                load_words("q", j)
-            if K_LAG <= j < ROUNDS + K_LAG:
-                load_words("k", j - K_LAG)
+            for w, r in (("q", j), ("k", j - K_LAG)):
+                if 0 <= r < ROUNDS:
+                    if r % SCALE_ROUNDS == 0:
+                        load_scales(w, r // SCALE_ROUNDS)
+                    load_words(w, r)
 
         def sort_words(r):
             x_sorted[r] = sorted_pool.tile([P, BATCH, ROUND, 2, P], F32, name="x_sorted")
@@ -193,12 +188,10 @@ def tile_multiheadattention_pa_k_kernel(
         masks.make_identity(nc, identity[:])
         nc.scalar.dma_start(out=cos_sb[:], in_=cos)
         nc.scalar.dma_start(out=sin_sb[:], in_=sin)
-        for group in range(ROUNDS // SCALE_ROUNDS):
+        for half in range(2):
             for w in weights:
                 nc.vector.memset(
-                    w_planes[w][
-                        :, group * SCALE_PASSES : (group + 1) * SCALE_PASSES, :
-                    ].bitcast(I32),
+                    w_planes[w][:, half * SCALE_PASSES : (half + 1) * SCALE_PASSES, :].bitcast(I32),
                     0,
                 )
 
@@ -206,9 +199,9 @@ def tile_multiheadattention_pa_k_kernel(
         for j in range(LOAD_AHEAD):
             load_step(j)
         sort_words(0)
+        sort_words(1)
         transpose_round(0)
         quantise_round(0)
-        sort_words(1)
 
         for s in range(ROUNDS + K_LAG):
             load_step(s + LOAD_AHEAD)
@@ -218,10 +211,10 @@ def tile_multiheadattention_pa_k_kernel(
                 multiply_round("q", s)
             if s >= K_LAG:
                 multiply_round("k", s - K_LAG)
-            if s + 1 < ROUNDS:
-                quantise_round(s + 1)
             if s + 2 < ROUNDS:
                 sort_words(s + 2)
+            if s + 1 < ROUNDS:
+                quantise_round(s + 1)
             if s == ROUNDS - 1:
                 rotate_and_store("q")
         rotate_and_store("k")

@@ -29,8 +29,7 @@ ROUND = 4
 ROUNDS = PASSES // ROUND
 K_LAG = 1
 LOAD_AHEAD = 3
-SCALE_ROUNDS = ROUNDS // 2
-SCALE_PASSES = SCALE_ROUNDS * ROUND
+SCALE_ROWS = K_PASS // 32
 
 FLOPS = 2 * BATCH * SEQ * D_MODEL * 2 * CHANNELS
 
@@ -83,13 +82,12 @@ def tile_multiheadattention_pa_k_kernel(
                     in_=x[b, :, r * ROUND * K_PASS : (r + 1) * ROUND * K_PASS],
                 )
 
-        def load_scales(w, half):
-            first = half * SCALE_PASSES
-            rows = scales_in[w].bitcast(I32).rearrange("g (qq r) n -> r qq g n", r=4)
-            for r4 in range(4):
+        def load_scales(w):
+            rows = scales_in[w].bitcast(I32).rearrange("g q n -> q g n")
+            for q in range(SCALE_ROWS):
+                live = 32 * (q // 4) + q % 4
                 nc.sync.dma_start(
-                    out=w_planes[w][r4:P:32, first : first + SCALE_PASSES, :].bitcast(I32),
-                    in_=rows[r4, :, first : first + SCALE_PASSES, :],
+                    out=w_planes[w][live : live + 1, :, :].bitcast(I32), in_=rows[q : q + 1, :, :]
                 )
 
         def load_words(w, r):
@@ -108,8 +106,8 @@ def tile_multiheadattention_pa_k_kernel(
                 load_x(j + 1)
             for w, r in (("q", j), ("k", j - K_LAG)):
                 if 0 <= r < ROUNDS:
-                    if r % SCALE_ROUNDS == 0:
-                        load_scales(w, r // SCALE_ROUNDS)
+                    if r == 0:
+                        load_scales(w)
                     load_words(w, r)
 
         def sort_words(r):
@@ -188,12 +186,8 @@ def tile_multiheadattention_pa_k_kernel(
         masks.make_identity(nc, identity[:])
         nc.scalar.dma_start(out=cos_sb[:], in_=cos)
         nc.scalar.dma_start(out=sin_sb[:], in_=sin)
-        for half in range(2):
-            for w in weights:
-                nc.vector.memset(
-                    w_planes[w][:, half * SCALE_PASSES : (half + 1) * SCALE_PASSES, :].bitcast(I32),
-                    0,
-                )
+        for w in weights:
+            nc.vector.memset(w_planes[w][:].bitcast(I32), 0)
 
         load_x(0)
         for j in range(LOAD_AHEAD):

@@ -84,11 +84,13 @@ def tile_multiheadattention_pa_k_kernel(
 
         def load_scales(w):
             rows = scales_in[w].bitcast(I32).rearrange("g q n -> q g n")
-            for q in range(SCALE_ROWS):
-                live = 32 * (q // 4) + q % 4
-                nc.sync.dma_start(
-                    out=w_planes[w][live : live + 1, :, :].bitcast(I32), in_=rows[q : q + 1, :, :]
-                )
+            for low in range(SCALE_ROWS // 2):
+                for q in (low, low + SCALE_ROWS // 2):
+                    live = 32 * (q // 4) + q % 4
+                    nc.sync.dma_start(
+                        out=w_planes[w][live : live + 1, :, :].bitcast(I32),
+                        in_=rows[q : q + 1, :, :],
+                    )
 
         def load_words(w, r):
             w_words[w, r] = words_pool.tile(

@@ -23,13 +23,13 @@ D_MODEL = 16384
 CHANNELS = 512
 HEAD = CHANNELS // 2
 PASSES = D_MODEL // K_PASS
-WORDS = K_PASS // 2
+SCALE_ROWS = K_PASS // 32
 
 ROUND = 4
 ROUNDS = PASSES // ROUND
-K_LAG = 1
 LOAD_AHEAD = 3
-SCALE_ROWS = K_PASS // 32
+QUANT = 2
+KEY_ROUNDS = 2
 
 FLOPS = 2 * BATCH * SEQ * D_MODEL * 2 * CHANNELS
 
@@ -48,11 +48,13 @@ def tile_multiheadattention_pa_k_kernel(
         x_pool = ctx.enter_context(tc.tile_pool(name="x_pool", bufs=LOAD_AHEAD + 1))
         sorted_pool = ctx.enter_context(tc.tile_pool(name="sorted_pool", bufs=3))
         grouped_pool = ctx.enter_context(tc.tile_pool(name="grouped_pool", bufs=2))
-        words_pool = ctx.enter_context(tc.tile_pool(name="words_pool", bufs=LOAD_AHEAD + 1))
+        wq_pool = ctx.enter_context(tc.tile_pool(name="wq_pool", bufs=LOAD_AHEAD + 1))
+        wk_pool = ctx.enter_context(tc.tile_pool(name="wk_pool", bufs=ROUNDS))
         rot_pool = ctx.enter_context(tc.tile_pool(name="rot_pool", bufs=2))
         sums_pool = ctx.enter_context(tc.psum_pool(name="sums_pool", bufs=1))
         xt_pool = ctx.enter_context(tc.psum_pool(name="xt_pool", bufs=ROUND))
         ctx.enter_context(tc.manual_schedule())
+        words_pool = {"q": wq_pool, "k": wk_pool}
 
         identity = keep.tile([P, P], F32, name="identity")
         cos_sb = keep.tile([P, HEAD], BF16, name="cos_sb")
@@ -93,7 +95,7 @@ def tile_multiheadattention_pa_k_kernel(
                     )
 
         def load_words(w, r):
-            w_words[w, r] = words_pool.tile(
+            w_words[w, r] = words_pool[w].tile(
                 [P, ROUND, 2 * CHANNELS], U8, name="words_" + w, align_bytes=64
             )
             nc.sync.dma_start(
@@ -103,14 +105,13 @@ def tile_multiheadattention_pa_k_kernel(
                 .rearrange("g p n -> p g n"),
             )
 
-        def load_step(j):
+        def load_for_query_step(j):
             if j + 1 < ROUNDS:
                 load_x(j + 1)
-            for w, r in (("q", j), ("k", j - K_LAG)):
-                if 0 <= r < ROUNDS:
-                    if r == 0:
-                        load_scales(w)
-                    load_words(w, r)
+            if j == 0:
+                load_scales("q")
+            if j < ROUNDS:
+                load_words("q", j)
 
         def sort_words(r):
             x_sorted[r] = sorted_pool.tile([P, BATCH, ROUND, 2, P], F32, name="x_sorted")
@@ -136,54 +137,45 @@ def tile_multiheadattention_pa_k_kernel(
                 )
 
         def quantise_round(r):
-            passes = slice(r * ROUND, (r + 1) * ROUND)
-            nc.vector.quantize_mx(
-                out=x_codes[:, passes].rearrange("p g b s -> p (g b s)").bitcast(FP8X4),
-                scales=x_scales[:, passes].rearrange("p g b s -> p (g b s)"),
-                in_=x_grouped[r][:].rearrange("p g b s t -> p (g b s t)"),
+            for first in range(0, ROUND, QUANT):
+                passes = slice(r * ROUND + first, r * ROUND + first + QUANT)
+                nc.vector.quantize_mx(
+                    out=x_codes[:, passes].rearrange("p g b s -> p (g b s)").bitcast(FP8X4),
+                    scales=x_scales[:, passes].rearrange("p g b s -> p (g b s)"),
+                    in_=x_grouped[r][:, first : first + QUANT].rearrange(
+                        "p g b s t -> p (g b s t)"
+                    ),
+                )
+
+        def multiply(w, g, b):
+            nc.tensor.matmul_mx(
+                out=sums[w, b][:],
+                lhsT=x_codes[:, g, b, :].bitcast(FP8X4),
+                lhsT_scale=x_scales[:, g, b, :],
+                rhs=w_words[w, g // ROUND][:, g % ROUND, :].bitcast(FP4X4),
+                rhs_scale=w_planes[w][:, g, :],
+                start=(g == 0),
+                stop=(g == PASSES - 1),
             )
 
-        def multiply_round(w, r):
-            for b in range(BATCH):
-                for g in range(r * ROUND, (r + 1) * ROUND):
-                    nc.tensor.matmul_mx(
-                        out=sums[w, b][:],
-                        lhsT=x_codes[:, g, b, :].bitcast(FP8X4),
-                        lhsT_scale=x_scales[:, g, b, :],
-                        rhs=w_words[w, r][:, g - r * ROUND, :].bitcast(FP4X4),
-                        rhs_scale=w_planes[w][:, g, :],
-                        start=(g == 0),
-                        stop=(g == PASSES - 1),
-                    )
-
-        def rotate_and_store(w):
-            by_cos = {}
-            by_sin = {}
-            for b in range(BATCH):
-                heads = sums[w, b][:].rearrange("s (h c) -> s h c", h=2)
-                by_cos[b] = rot_pool.tile([P, 2, HEAD], F32, name="by_cos")
-                by_sin[b] = rot_pool.tile([P, 2, HEAD], F32, name="by_sin")
-                nc.vector.tensor_tensor(
-                    out=by_cos[b][:],
-                    in0=heads,
-                    in1=cos_sb[:].unsqueeze(1).to_broadcast([P, 2, HEAD]),
-                    op=MULT,
-                )
-                nc.vector.tensor_tensor(
-                    out=by_sin[b][:],
-                    in0=heads,
-                    in1=sin_sb[:].unsqueeze(1).to_broadcast([P, 2, HEAD]),
-                    op=MULT,
-                )
-            for b in range(BATCH):
-                rotated = rot_pool.tile([P, 2, HEAD], F32, name="rotated")
-                nc.vector.tensor_tensor(
-                    out=rotated[:, 0, :], in0=by_cos[b][:, 0, :], in1=by_sin[b][:, 1, :], op=SUBTRACT
-                )
-                nc.vector.tensor_tensor(
-                    out=rotated[:, 1, :], in0=by_cos[b][:, 1, :], in1=by_sin[b][:, 0, :], op=ADD
-                )
-                nc.sync.dma_start(out=outputs[w][b].rearrange("h s c -> s h c"), in_=rotated[:])
+        def rotate_and_store(w, b):
+            heads = sums[w, b][:].rearrange("s (h c) -> s h c", h=2)
+            by_cos = rot_pool.tile([P, 2, HEAD], F32, name="by_cos")
+            by_sin = rot_pool.tile([P, 2, HEAD], F32, name="by_sin")
+            rotated = rot_pool.tile([P, 2, HEAD], F32, name="rotated")
+            nc.vector.tensor_tensor(
+                out=by_cos[:], in0=heads, in1=cos_sb[:].unsqueeze(1).to_broadcast([P, 2, HEAD]), op=MULT
+            )
+            nc.vector.tensor_tensor(
+                out=by_sin[:], in0=heads, in1=sin_sb[:].unsqueeze(1).to_broadcast([P, 2, HEAD]), op=MULT
+            )
+            nc.vector.tensor_tensor(
+                out=rotated[:, 0, :], in0=by_cos[:, 0, :], in1=by_sin[:, 1, :], op=SUBTRACT
+            )
+            nc.vector.tensor_tensor(
+                out=rotated[:, 1, :], in0=by_cos[:, 1, :], in1=by_sin[:, 0, :], op=ADD
+            )
+            nc.sync.dma_start(out=outputs[w][b].rearrange("h s c -> s h c"), in_=rotated[:])
 
         masks.make_identity(nc, identity[:])
         nc.scalar.dma_start(out=cos_sb[:], in_=cos)
@@ -193,24 +185,32 @@ def tile_multiheadattention_pa_k_kernel(
 
         load_x(0)
         for j in range(LOAD_AHEAD):
-            load_step(j)
+            load_for_query_step(j)
         sort_words(0)
         sort_words(1)
         transpose_round(0)
         quantise_round(0)
 
-        for s in range(ROUNDS + K_LAG):
-            load_step(s + LOAD_AHEAD)
+        for s in range(ROUNDS):
+            load_for_query_step(s + LOAD_AHEAD)
             if s + 1 < ROUNDS:
                 transpose_round(s + 1)
-            if s < ROUNDS:
-                multiply_round("q", s)
-            if s >= K_LAG:
-                multiply_round("k", s - K_LAG)
+            for g in range(s * ROUND, (s + 1) * ROUND):
+                for b in range(BATCH):
+                    multiply("q", g, b)
             if s + 2 < ROUNDS:
                 sort_words(s + 2)
             if s + 1 < ROUNDS:
                 quantise_round(s + 1)
-            if s == ROUNDS - 1:
-                rotate_and_store("q")
-        rotate_and_store("k")
+
+        load_scales("k")
+        for r in range(ROUNDS):
+            load_words("k", r)
+        for b in range(BATCH):
+            rotate_and_store("q", b)
+        for first in range(0, PASSES, KEY_ROUNDS * ROUND):
+            for b in range(BATCH):
+                for g in range(first, first + KEY_ROUNDS * ROUND):
+                    multiply("k", g, b)
+        for b in range(BATCH):
+            rotate_and_store("k", b)

@@ -78,11 +78,10 @@ def tile_multiheadattention_pa_k_kernel(
 
         def load_x(r):
             x_raw[r] = x_pool.tile([P, BATCH, ROUND * K_PASS], BF16, name="x_raw")
-            for b in range(BATCH):
-                nc.sync.dma_start(
-                    out=x_raw[r][:, b, :],
-                    in_=x[b, :, r * ROUND * K_PASS : (r + 1) * ROUND * K_PASS],
-                )
+            nc.sync.dma_start(
+                out=x_raw[r][:],
+                in_=x[:, :, r * ROUND * K_PASS : (r + 1) * ROUND * K_PASS].rearrange("b s k -> s b k"),
+            )
 
         def load_scales(w):
             rows = scales_in[w].bitcast(I32).rearrange("g q n -> q g n")
@@ -172,14 +171,13 @@ def tile_multiheadattention_pa_k_kernel(
             nc.vector.tensor_tensor(
                 out=rotated[:, 0, :], in0=by_cos[:, 0, :], in1=by_sin[:, 1, :], op=SUBTRACT
             )
+            nc.sync.dma_start(out=outputs[w][b, 0], in_=rotated[:, 0, :])
             nc.vector.tensor_tensor(
                 out=rotated[:, 1, :], in0=by_cos[:, 1, :], in1=by_sin[:, 0, :], op=ADD
             )
-            nc.sync.dma_start(out=outputs[w][b].rearrange("h s c -> s h c"), in_=rotated[:])
+            nc.sync.dma_start(out=outputs[w][b, 1], in_=rotated[:, 1, :])
 
         masks.make_identity(nc, identity[:])
-        nc.scalar.dma_start(out=cos_sb[:], in_=cos)
-        nc.scalar.dma_start(out=sin_sb[:], in_=sin)
         for w in weights:
             nc.vector.memset(w_planes[w][:].bitcast(I32), 0)
 
@@ -206,6 +204,8 @@ def tile_multiheadattention_pa_k_kernel(
         load_scales("k")
         for r in range(ROUNDS):
             load_words("k", r)
+        nc.sync.dma_start(out=cos_sb[:], in_=cos)
+        nc.sync.dma_start(out=sin_sb[:], in_=sin)
         for b in range(BATCH):
             rotate_and_store("q", b)
         for first in range(0, PASSES, KEY_ROUNDS * ROUND):

@@ -27,9 +27,10 @@ SCALE_ROWS = K_PASS // 32
 
 ROUND = 4
 ROUNDS = PASSES // ROUND
-LOAD_AHEAD = 3
+X_BUFS = 5
+BUNDLES_AHEAD = 4
 QUANT = 2
-KEY_ROUNDS = 2
+PIECE = 8
 
 FLOPS = 2 * BATCH * SEQ * D_MODEL * 2 * CHANNELS
 
@@ -45,16 +46,14 @@ def tile_multiheadattention_pa_k_kernel(
 
     with ExitStack() as ctx:
         keep = ctx.enter_context(tc.tile_pool(name="keep", bufs=1))
-        x_pool = ctx.enter_context(tc.tile_pool(name="x_pool", bufs=LOAD_AHEAD + 1))
-        sorted_pool = ctx.enter_context(tc.tile_pool(name="sorted_pool", bufs=3))
+        x_pool = ctx.enter_context(tc.tile_pool(name="x_pool", bufs=X_BUFS))
+        sorted_pool = ctx.enter_context(tc.tile_pool(name="sorted_pool", bufs=2))
         grouped_pool = ctx.enter_context(tc.tile_pool(name="grouped_pool", bufs=2))
-        wq_pool = ctx.enter_context(tc.tile_pool(name="wq_pool", bufs=LOAD_AHEAD + 1))
-        wk_pool = ctx.enter_context(tc.tile_pool(name="wk_pool", bufs=ROUNDS))
+        words_pool = ctx.enter_context(tc.tile_pool(name="words_pool", bufs=ROUNDS))
         rot_pool = ctx.enter_context(tc.tile_pool(name="rot_pool", bufs=2))
         sums_pool = ctx.enter_context(tc.psum_pool(name="sums_pool", bufs=1))
         xt_pool = ctx.enter_context(tc.psum_pool(name="xt_pool", bufs=ROUND))
         ctx.enter_context(tc.manual_schedule())
-        words_pool = {"q": wq_pool, "k": wk_pool}
 
         identity = keep.tile([P, P], F32, name="identity")
         cos_sb = keep.tile([P, HEAD], BF16, name="cos_sb")
@@ -62,8 +61,9 @@ def tile_multiheadattention_pa_k_kernel(
         x_codes = keep.tile([P, PASSES, BATCH, SEQ], U32, name="x_codes", align_bytes=64)
         x_scales = keep.tile([P, PASSES, BATCH, SEQ], U8, name="x_scales", align_bytes=64)
         w_planes = {
-            w: keep.tile([P, PASSES, CHANNELS], U8, name="planes_" + w, align_bytes=64)
+            (w, i): keep.tile([P, PIECE, CHANNELS], U8, name="planes_%s%d" % (w, i), align_bytes=64)
             for w in weights
+            for i in range(PASSES // PIECE)
         }
         sums = {
             (w, b): sums_pool.tile([P, CHANNELS], F32, name="sums_%s%d" % (w, b))
@@ -83,18 +83,20 @@ def tile_multiheadattention_pa_k_kernel(
                 in_=x[:, :, r * ROUND * K_PASS : (r + 1) * ROUND * K_PASS].rearrange("b s k -> s b k"),
             )
 
-        def load_scales(w):
+        def zero_planes(first):
+            for w in weights:
+                nc.vector.memset(w_planes[w, first // PIECE][:].bitcast(I32), 0)
+
+        def load_scales(w, first):
             rows = scales_in[w].bitcast(I32).rearrange("g q n -> q g n")
-            for low in range(SCALE_ROWS // 2):
-                for q in (low, low + SCALE_ROWS // 2):
-                    live = 32 * (q // 4) + q % 4
-                    nc.sync.dma_start(
-                        out=w_planes[w][live : live + 1, :, :].bitcast(I32),
-                        in_=rows[q : q + 1, :, :],
-                    )
+            for r in range(4):
+                nc.sync.dma_start(
+                    out=w_planes[w, first // PIECE][r:P:32, :, :].bitcast(I32),
+                    in_=rows[r:SCALE_ROWS:4, first : first + PIECE, :],
+                )
 
         def load_words(w, r):
-            w_words[w, r] = words_pool[w].tile(
+            w_words[w, r] = words_pool.tile(
                 [P, ROUND, 2 * CHANNELS], U8, name="words_" + w, align_bytes=64
             )
             nc.sync.dma_start(
@@ -104,13 +106,28 @@ def tile_multiheadattention_pa_k_kernel(
                 .rearrange("g p n -> p g n"),
             )
 
-        def load_for_query_step(j):
+        def load_bundle(j):
+            if j >= ROUNDS:
+                return
+            new_piece = (j * ROUND) % PIECE == 0
             if j + 1 < ROUNDS:
                 load_x(j + 1)
-            if j == 0:
-                load_scales("q")
-            if j < ROUNDS:
+            if j == ROUNDS - 1:
+                return
+            if j == ROUNDS - 2:
+                load_scales("q", j * ROUND)
                 load_words("q", j)
+                load_words("q", j + 1)
+                load_scales("k", j * ROUND)
+                load_words("k", j)
+                load_words("k", j + 1)
+                nc.sync.dma_start(out=cos_sb[:], in_=cos)
+                nc.sync.dma_start(out=sin_sb[:], in_=sin)
+                return
+            for w in weights:
+                if new_piece:
+                    load_scales(w, j * ROUND)
+                load_words(w, j)
 
         def sort_words(r):
             x_sorted[r] = sorted_pool.tile([P, BATCH, ROUND, 2, P], F32, name="x_sorted")
@@ -152,10 +169,15 @@ def tile_multiheadattention_pa_k_kernel(
                 lhsT=x_codes[:, g, b, :].bitcast(FP8X4),
                 lhsT_scale=x_scales[:, g, b, :],
                 rhs=w_words[w, g // ROUND][:, g % ROUND, :].bitcast(FP4X4),
-                rhs_scale=w_planes[w][:, g, :],
+                rhs_scale=w_planes[w, g // PIECE][:, g % PIECE, :],
                 start=(g == 0),
                 stop=(g == PASSES - 1),
             )
+
+        def multiply_round(w, r):
+            for g in range(r * ROUND, (r + 1) * ROUND):
+                for b in range(BATCH):
+                    multiply(w, g, b)
 
         def rotate_and_store(w, b):
             heads = sums[w, b][:].rearrange("s (h c) -> s h c", h=2)
@@ -178,39 +200,37 @@ def tile_multiheadattention_pa_k_kernel(
             nc.sync.dma_start(out=outputs[w][b, 1], in_=rotated[:, 1, :])
 
         masks.make_identity(nc, identity[:])
-        for w in weights:
-            nc.vector.memset(w_planes[w][:].bitcast(I32), 0)
+        zero_planes(0)
+        zero_planes(PIECE)
 
         load_x(0)
-        for j in range(LOAD_AHEAD):
-            load_for_query_step(j)
+        for j in range(BUNDLES_AHEAD):
+            load_bundle(j)
         sort_words(0)
-        sort_words(1)
         transpose_round(0)
+        sort_words(1)
         quantise_round(0)
+        zero_planes(2 * PIECE)
 
-        for s in range(ROUNDS):
-            load_for_query_step(s + LOAD_AHEAD)
-            if s + 1 < ROUNDS:
-                transpose_round(s + 1)
-            for g in range(s * ROUND, (s + 1) * ROUND):
-                for b in range(BATCH):
-                    multiply("q", g, b)
-            if s + 2 < ROUNDS:
-                sort_words(s + 2)
-            if s + 1 < ROUNDS:
-                quantise_round(s + 1)
+        for s in range(ROUNDS - 2):
+            load_bundle(s + BUNDLES_AHEAD)
+            transpose_round(s + 1)
+            multiply_round("q", s)
+            multiply_round("k", s)
+            quantise_round(s + 1)
+            sort_words(s + 2)
+            if s == 0:
+                zero_planes(3 * PIECE)
 
-        load_scales("k")
-        for r in range(ROUNDS):
-            load_words("k", r)
-        nc.sync.dma_start(out=cos_sb[:], in_=cos)
-        nc.sync.dma_start(out=sin_sb[:], in_=sin)
+        last = ROUNDS - 1
+        transpose_round(last)
+        multiply_round("q", last - 1)
+        quantise_round(last)
+        multiply_round("q", last)
         for b in range(BATCH):
             rotate_and_store("q", b)
-        for first in range(0, PASSES, KEY_ROUNDS * ROUND):
-            for b in range(BATCH):
-                for g in range(first, first + KEY_ROUNDS * ROUND):
-                    multiply("k", g, b)
+        for b in range(BATCH):
+            for g in range((last - 1) * ROUND, PASSES):
+                multiply("k", g, b)
         for b in range(BATCH):
             rotate_and_store("k", b)

@@ -31,6 +31,7 @@ X_BUFS = 5
 BUNDLES_AHEAD = 4
 QUANT = 2
 PIECE = 8
+WARM_UP = 12
 
 FLOPS = 2 * BATCH * SEQ * D_MODEL * 2 * CHANNELS
 
@@ -200,6 +201,9 @@ def tile_multiheadattention_pa_k_kernel(
             nc.sync.dma_start(out=outputs[w][b, 1], in_=rotated[:, 1, :])
 
         masks.make_identity(nc, identity[:])
+        warm = xt_pool.tile([P, BATCH, 2, SEQ], F32, name="xt")
+        for i in range(WARM_UP):
+            nc.tensor.matmul(warm[:, 0, 0, :], lhsT=identity[:], rhs=identity[:], start=True, stop=True)
         zero_planes(0)
         zero_planes(PIECE)
 
@@ -216,21 +220,22 @@ def tile_multiheadattention_pa_k_kernel(
             load_bundle(s + BUNDLES_AHEAD)
             transpose_round(s + 1)
             multiply_round("q", s)
-            multiply_round("k", s)
-            quantise_round(s + 1)
-            sort_words(s + 2)
+            if s < ROUNDS - 3:
+                multiply_round("k", s)
+                quantise_round(s + 1)
+                sort_words(s + 2)
+            else:
+                sort_words(s + 2)
+                quantise_round(s + 1)
             if s == 0:
                 zero_planes(3 * PIECE)
 
         last = ROUNDS - 1
         transpose_round(last)
-        multiply_round("q", last - 1)
+        multiply_round("k", last - 2)
         quantise_round(last)
-        multiply_round("q", last)
-        for b in range(BATCH):
-            rotate_and_store("q", b)
-        for b in range(BATCH):
-            for g in range((last - 1) * ROUND, PASSES):
-                multiply("k", g, b)
-        for b in range(BATCH):
-            rotate_and_store("k", b)
+        for w in weights:
+            for b in range(BATCH):
+                for g in range((last - 1) * ROUND, PASSES):
+                    multiply(w, g, b)
+                rotate_and_store(w, b)

@@ -122,13 +122,14 @@ def tile_multiheadattention_pa_k_kernel(
                 load_scales("k", j * ROUND)
                 load_words("k", j)
                 load_words("k", j + 1)
-                nc.sync.dma_start(out=cos_sb[:], in_=cos)
-                nc.sync.dma_start(out=sin_sb[:], in_=sin)
                 return
             for w in weights:
                 if new_piece:
                     load_scales(w, j * ROUND)
                 load_words(w, j)
+            if j == ROUNDS // 2:
+                nc.sync.dma_start(out=cos_sb[:], in_=cos)
+                nc.sync.dma_start(out=sin_sb[:], in_=sin)
 
         def sort_words(r):
             x_sorted[r] = sorted_pool.tile([P, BATCH, ROUND, 2, P], F32, name="x_sorted")

@@ -48,7 +48,6 @@ def tile_multiheadattention_pa_k_kernel(
     with ExitStack() as ctx:
         keep = ctx.enter_context(tc.tile_pool(name="keep", bufs=1))
         x_pool = ctx.enter_context(tc.tile_pool(name="x_pool", bufs=X_BUFS))
-        sorted_pool = ctx.enter_context(tc.tile_pool(name="sorted_pool", bufs=2))
         grouped_pool = ctx.enter_context(tc.tile_pool(name="grouped_pool", bufs=2))
         words_pool = ctx.enter_context(tc.tile_pool(name="words_pool", bufs=ROUNDS))
         rot_pool = ctx.enter_context(tc.tile_pool(name="rot_pool", bufs=2))
@@ -73,7 +72,6 @@ def tile_multiheadattention_pa_k_kernel(
         }
 
         x_raw = {}
-        x_sorted = {}
         x_grouped = {}
         w_words = {}
 
@@ -131,25 +129,19 @@ def tile_multiheadattention_pa_k_kernel(
                 nc.sync.dma_start(out=cos_sb[:], in_=cos)
                 nc.sync.dma_start(out=sin_sb[:], in_=sin)
 
-        def sort_words(r):
-            x_sorted[r] = sorted_pool.tile([P, BATCH, ROUND, 2, P], F32, name="x_sorted")
-            nc.vector.tensor_copy(
-                out=x_sorted[r][:],
-                in_=x_raw[r][:]
-                .bitcast(F32)
-                .rearrange("s b (g p u) -> s b g u p", g=ROUND, u=2),
-            )
-
         def transpose_round(r):
             x_grouped[r] = grouped_pool.tile(
                 [P, ROUND, BATCH, SEQ, PACK], BF16, name="x_grouped", align_bytes=64
             )
             grouped_words = x_grouped[r][:].bitcast(F32)
+            words = x_raw[r][:].bitcast(F32)
             for g in range(ROUND):
                 xt = xt_pool.tile([P, BATCH, 2, SEQ], F32, name="xt")
                 for b in range(BATCH):
                     for u in range(2):
-                        nc.tensor.transpose(xt[:, b, u, :], x_sorted[r][:, b, g, u, :], identity[:])
+                        nc.tensor.transpose(
+                            xt[:, b, u, :], words[:, b, 2 * P * g + u : 2 * P * (g + 1) : 2], identity[:]
+                        )
                 nc.scalar.copy(
                     out=grouped_words[:, g], in_=xt[:].rearrange("p b u s -> p b s u")
                 )
@@ -211,9 +203,7 @@ def tile_multiheadattention_pa_k_kernel(
         load_x(0)
         for j in range(BUNDLES_AHEAD):
             load_bundle(j)
-        sort_words(0)
         transpose_round(0)
-        sort_words(1)
         quantise_round(0)
         zero_planes(2 * PIECE)
 
@@ -224,9 +214,7 @@ def tile_multiheadattention_pa_k_kernel(
             if s < ROUNDS - 3:
                 multiply_round("k", s)
                 quantise_round(s + 1)
-                sort_words(s + 2)
             else:
-                sort_words(s + 2)
                 quantise_round(s + 1)
             if s == 0:
                 zero_planes(3 * PIECE)

@@ -142,9 +142,14 @@ def tile_multiheadattention_pa_k_kernel(
                         nc.tensor.transpose(
                             xt[:, b, u, :], words[:, b, 2 * P * g + u : 2 * P * (g + 1) : 2], identity[:]
                         )
-                nc.scalar.copy(
-                    out=grouped_words[:, g], in_=xt[:].rearrange("p b u s -> p b s u")
-                )
+                if g % 2 == 0:
+                    nc.scalar.copy(
+                        out=grouped_words[:, g], in_=xt[:].rearrange("p b u s -> p b s u")
+                    )
+                else:
+                    nc.vector.tensor_copy(
+                        out=grouped_words[:, g], in_=xt[:].rearrange("p b u s -> p b s u")
+                    )
 
         def quantise_round(r):
             for first in range(0, ROUND, QUANT):

from contextlib import ExitStack

import concourse.masks as masks
import concourse.mybir as mybir

F32 = mybir.dt.float32
BF16 = mybir.dt.bfloat16
I32 = mybir.dt.int32
U32 = mybir.dt.uint32
U8 = mybir.dt.uint8
FP8X4 = mybir.dt.float8_e4m3fn_x4
FP4X4 = mybir.dt.float4_e2m1fn_x4
MULT = mybir.AluOpType.mult
ADD = mybir.AluOpType.add
SUBTRACT = mybir.AluOpType.subtract

P = 128
PACK = 4
K_PASS = P * PACK
BATCH = 2
SEQ = 128
D_MODEL = 16384
CHANNELS = 512
HEAD = CHANNELS // 2
PASSES = D_MODEL // K_PASS
SCALE_ROWS = K_PASS // 32

ROUND = 4
ROUNDS = PASSES // ROUND
X_BUFS = 5
BUNDLES_AHEAD = 4
QUANT = 2
PIECE = 8
WARM_UP = 12

FLOPS = 2 * BATCH * SEQ * D_MODEL * 2 * CHANNELS


def tile_multiheadattention_pa_k_kernel(
    tc, x, wq_words, wq_scales, wk_words, wk_scales, cos, sin, out_0, out_1
):
    nc = tc.nc
    weights = ("q", "k")
    words_in = {"q": wq_words, "k": wk_words}
    scales_in = {"q": wq_scales, "k": wk_scales}
    outputs = {"q": out_0, "k": out_1}

    with ExitStack() as ctx:
        keep = ctx.enter_context(tc.tile_pool(name="keep", bufs=1))
        x_pool = ctx.enter_context(tc.tile_pool(name="x_pool", bufs=X_BUFS))
        grouped_pool = ctx.enter_context(tc.tile_pool(name="grouped_pool", bufs=2))
        words_pool = ctx.enter_context(tc.tile_pool(name="words_pool", bufs=ROUNDS))
        rot_pool = ctx.enter_context(tc.tile_pool(name="rot_pool", bufs=2))
        sums_pool = ctx.enter_context(tc.psum_pool(name="sums_pool", bufs=1))
        xt_pool = ctx.enter_context(tc.psum_pool(name="xt_pool", bufs=ROUND))
        ctx.enter_context(tc.manual_schedule())

        identity = keep.tile([P, P], F32, name="identity")
        cos_sb = keep.tile([P, HEAD], BF16, name="cos_sb")
        sin_sb = keep.tile([P, HEAD], BF16, name="sin_sb")
        x_codes = keep.tile([P, PASSES, BATCH, SEQ], U32, name="x_codes", align_bytes=64)
        x_scales = keep.tile([P, PASSES, BATCH, SEQ], U8, name="x_scales", align_bytes=64)
        w_planes = {
            (w, i): keep.tile([P, PIECE, CHANNELS], U8, name="planes_%s%d" % (w, i), align_bytes=64)
            for w in weights
            for i in range(PASSES // PIECE)
        }
        sums = {
            (w, b): sums_pool.tile([P, CHANNELS], F32, name="sums_%s%d" % (w, b))
            for w in weights
            for b in range(BATCH)
        }

        x_raw = {}
        x_grouped = {}
        w_words = {}

        def load_x(r):
            x_raw[r] = x_pool.tile([P, BATCH, ROUND * K_PASS], BF16, name="x_raw")
            nc.sync.dma_start(
                out=x_raw[r][:],
                in_=x[:, :, r * ROUND * K_PASS : (r + 1) * ROUND * K_PASS].rearrange("b s k -> s b k"),
            )

        def zero_planes(first):
            for w in weights:
                nc.vector.memset(w_planes[w, first // PIECE][:].bitcast(I32), 0)

        def load_scales(w, first):
            rows = scales_in[w].bitcast(I32).rearrange("g q n -> q g n")
            for r in range(4):
                nc.sync.dma_start(
                    out=w_planes[w, first // PIECE][r:P:32, :, :].bitcast(I32),
                    in_=rows[r:SCALE_ROWS:4, first : first + PIECE, :],
                )

        def load_words(w, r):
            w_words[w, r] = words_pool.tile(
                [P, ROUND, 2 * CHANNELS], U8, name="words_" + w, align_bytes=64
            )
            nc.sync.dma_start(
                out=w_words[w, r][:].bitcast(I32),
                in_=words_in[w][r * ROUND : (r + 1) * ROUND]
                .bitcast(I32)
                .rearrange("g p n -> p g n"),
            )

        def load_bundle(j):
            if j >= ROUNDS:
                return
            new_piece = (j * ROUND) % PIECE == 0
            if j + 1 < ROUNDS:
                load_x(j + 1)
            if j == ROUNDS - 1:
                return
            if j == ROUNDS - 2:
                load_scales("q", j * ROUND)
                load_words("q", j)
                load_words("q", j + 1)
                load_scales("k", j * ROUND)
                load_words("k", j)
                load_words("k", j + 1)
                return
            for w in weights:
                if new_piece:
                    load_scales(w, j * ROUND)
                load_words(w, j)
            if j == ROUNDS // 2:
                nc.sync.dma_start(out=cos_sb[:], in_=cos)
                nc.sync.dma_start(out=sin_sb[:], in_=sin)

        def transpose_round(r):
            x_grouped[r] = grouped_pool.tile(
                [P, ROUND, BATCH, SEQ, PACK], BF16, name="x_grouped", align_bytes=64
            )
            grouped_words = x_grouped[r][:].bitcast(F32)
            words = x_raw[r][:].bitcast(F32)
            for g in range(ROUND):
                xt = xt_pool.tile([P, BATCH, 2, SEQ], F32, name="xt")
                for b in range(BATCH):
                    for u in range(2):
                        nc.tensor.transpose(
                            xt[:, b, u, :], words[:, b, 2 * P * g + u : 2 * P * (g + 1) : 2], identity[:]
                        )
                if g % 2 == 0:
                    nc.scalar.copy(
                        out=grouped_words[:, g], in_=xt[:].rearrange("p b u s -> p b s u")
                    )
                else:
                    nc.vector.tensor_copy(
                        out=grouped_words[:, g], in_=xt[:].rearrange("p b u s -> p b s u")
                    )

        def quantise_round(r):
            for first in range(0, ROUND, QUANT):
                passes = slice(r * ROUND + first, r * ROUND + first + QUANT)
                nc.vector.quantize_mx(
                    out=x_codes[:, passes].rearrange("p g b s -> p (g b s)").bitcast(FP8X4),
                    scales=x_scales[:, passes].rearrange("p g b s -> p (g b s)"),
                    in_=x_grouped[r][:, first : first + QUANT].rearrange(
                        "p g b s t -> p (g b s t)"
                    ),
                )

        def multiply(w, g, b):
            nc.tensor.matmul_mx(
                out=sums[w, b][:],
                lhsT=x_codes[:, g, b, :].bitcast(FP8X4),
                lhsT_scale=x_scales[:, g, b, :],
                rhs=w_words[w, g // ROUND][:, g % ROUND, :].bitcast(FP4X4),
                rhs_scale=w_planes[w, g // PIECE][:, g % PIECE, :],
                start=(g == 0),
                stop=(g == PASSES - 1),
            )

        def multiply_round(w, r):
            for g in range(r * ROUND, (r + 1) * ROUND):
                for b in range(BATCH):
                    multiply(w, g, b)

        def rotate_and_store(w, b):
            heads = sums[w, b][:].rearrange("s (h c) -> s h c", h=2)
            by_cos = rot_pool.tile([P, 2, HEAD], F32, name="by_cos")
            by_sin = rot_pool.tile([P, 2, HEAD], F32, name="by_sin")
            rotated = rot_pool.tile([P, 2, HEAD], F32, name="rotated")
            nc.vector.tensor_tensor(
                out=by_cos[:], in0=heads, in1=cos_sb[:].unsqueeze(1).to_broadcast([P, 2, HEAD]), op=MULT
            )
            nc.vector.tensor_tensor(
                out=by_sin[:], in0=heads, in1=sin_sb[:].unsqueeze(1).to_broadcast([P, 2, HEAD]), op=MULT
            )
            nc.vector.tensor_tensor(
                out=rotated[:, 0, :], in0=by_cos[:, 0, :], in1=by_sin[:, 1, :], op=SUBTRACT
            )
            nc.sync.dma_start(out=outputs[w][b, 0], in_=rotated[:, 0, :])
            nc.vector.tensor_tensor(
                out=rotated[:, 1, :], in0=by_cos[:, 1, :], in1=by_sin[:, 0, :], op=ADD
            )
            nc.sync.dma_start(out=outputs[w][b, 1], in_=rotated[:, 1, :])

        masks.make_identity(nc, identity[:])
        warm = xt_pool.tile([P, BATCH, 2, SEQ], F32, name="xt")
        for i in range(WARM_UP):
            nc.tensor.matmul(warm[:, 0, 0, :], lhsT=identity[:], rhs=identity[:], start=True, stop=True)
        zero_planes(0)
        zero_planes(PIECE)

        load_x(0)
        for j in range(BUNDLES_AHEAD):
            load_bundle(j)
        transpose_round(0)
        quantise_round(0)
        zero_planes(2 * PIECE)

        for s in range(ROUNDS - 2):
            load_bundle(s + BUNDLES_AHEAD)
            transpose_round(s + 1)
            multiply_round("q", s)
            if s < ROUNDS - 3:
                multiply_round("k", s)
                quantise_round(s + 1)
            else:
                quantise_round(s + 1)
            if s == 0:
                zero_planes(3 * PIECE)

        last = ROUNDS - 1
        transpose_round(last)
        multiply_round("k", last - 2)
        quantise_round(last)
        for w in weights:
            for b in range(BATCH):
                for g in range((last - 1) * ROUND, PASSES):
                    multiply(w, g, b)
                rotate_and_store(w, b)
